import numpy as np
import ml_dtypes


def mxq(x, axis, fmt="e4m3"):
    dtype, down = {"e4m3": (ml_dtypes.float8_e4m3fn, 7), "e5m2": (ml_dtypes.float8_e5m2, 14)}[fmt]
    v = np.moveaxis(np.asarray(x, np.float32).astype(ml_dtypes.bfloat16).astype(np.float64), axis, -1)
    blocks = v.reshape(v.shape[:-1] + (-1, 32))
    amax = np.abs(blocks).max(-1, keepdims=True)
    byte = np.maximum(np.where(amax > 0, np.frexp(amax)[1] - 1 + 127, 0) - down, 1)
    scale = np.exp2(byte - 127.0)
    codes = (blocks / scale).astype(np.float32).astype(dtype).astype(np.float64)
    return np.moveaxis((codes * scale).reshape(v.shape), -1, axis)


WIDE = False


def mx_kscale(k):
    if not WIDE:
        return np.ones(k)
    levels = np.array([10, -10, 5, -5, 0])
    a = np.random.permutation(np.resize(levels, k // 512 * 4)).reshape(k // 512, 4)
    idx = np.arange(k)
    return np.exp2(a[idx // 512, idx % 128 // 32])


BF16 = ml_dtypes.bfloat16


def bf(x):
    return np.asarray(x, np.float32).astype(BF16)


def f64(x):
    return np.asarray(x).astype(np.float64)


B, H, W, C, NH, WS, SHIFT, F = 4, 16, 16, 1024, 32, 8, 3, 4096
S = WS * WS
HD = C // NH
EPS = 1e-5


def layer_norm(x, w, b):
    m = x.mean(-1, keepdims=True)
    v = ((x - m) ** 2).mean(-1, keepdims=True)
    return (x - m) / np.sqrt(v + EPS) * w + b


def to_heads(t):
    return t.reshape(-1, S, NH, HD).transpose(0, 2, 1, 3)


def setup_inputs():
    s = mx_kscale(C)
    return {"x": bf(np.random.standard_normal((B, H * W, C))),
            "norm1_w": bf((1.0 + 0.1 * np.random.standard_normal(C)) * s),
            "norm1_b": bf(0.1 * np.random.standard_normal(C) * s),
            "qkv_w": bf(np.random.standard_normal((3 * C, C)) / np.sqrt(C) / s[None, :]),
            "qkv_b": bf(0.1 * np.random.standard_normal(3 * C))}


def reference(x, norm1_w, norm1_b, qkv_w, qkv_b):
    h = layer_norm(f64(x), f64(norm1_w), f64(norm1_b)).reshape(B, H, W, C)
    h = np.roll(h, (-SHIFT, -SHIFT), axis=(1, 2))
    win = h.reshape(B, H // WS, WS, W // WS, WS, C)
    win = win.transpose(0, 1, 3, 2, 4, 5).reshape(-1, S, C)
    win = win
    qkv = (mxq(win, 2, "e4m3") @ mxq(f64(qkv_w), 1, "e4m3").T) + f64(qkv_b)
    q, k, v = np.split(qkv, 3, axis=-1)
    return to_heads(q), to_heads(k), to_heads(v)

@@ -1,0 +1,241 @@
+from contextlib import ExitStack
+
+import concourse.mybir as mybir
+from concourse.masks import make_identity
+
+F32 = mybir.dt.float32
+BF16 = mybir.dt.bfloat16
+U32 = mybir.dt.uint32
+U8 = mybir.dt.uint8
+FP8X4 = mybir.dt.float8_e4m3fn_x4
+ALU = mybir.AluOpType
+ACT = mybir.ActivationFunctionType
+
+P = 128
+C = 1024
+EPS = 1e-5
+IMAGES, GRID, WS, SHIFT = 4, 16, 8, 3
+HD = 32
+PACK = 4
+PASSES = C // (P * PACK)
+QUARTERS = C // (2 * P)
+N_COLS = 512
+N_CHUNKS = 3 * C // N_COLS
+HEADS = N_COLS // HD
+ROW_TILES = N_COLS // P
+PAIR = 2
+SCALAR_EVERY = 4
+
+FLOPS = 2 * IMAGES * GRID * GRID * C * 3 * C
+
+
+def tile_swintransformerblock_pa_kernel(
+    tc, x, norm1_w, norm1_b, qkv_w, qkv_b, out_0, out_1, out_2
+):
+    nc = tc.nc
+    outs = (out_0, out_1, out_2)
+
+    with ExitStack() as ctx:
+        const = ctx.enter_context(tc.tile_pool(name="const", bufs=1))
+        small = ctx.enter_context(tc.tile_pool(name="small", bufs=4))
+        work = ctx.enter_context(tc.tile_pool(name="work", bufs=2))
+        stage_pool = ctx.enter_context(tc.tile_pool(name="stage", bufs=3))
+        flip_pool = ctx.enter_context(tc.psum_pool(name="flip", bufs=4))
+        acc_pool = ctx.enter_context(tc.psum_pool(name="acc", bufs=4))
+
+        x_raw = const.tile([P, WS, C], BF16)
+        x_rows = x.rearrange("b (q e) k -> (b q) e k", e=WS)
+        for pair in range(WS // PAIR):
+            tiles = slice(PAIR * pair, PAIR * (pair + 1))
+            nc.sync.dma_start(out=x_raw[:, tiles, :], in_=x_rows[:, tiles, :])
+
+        gain_bf = const.tile([P, QUARTERS, 2], BF16)
+        beta_bf = const.tile([P, QUARTERS, 2], BF16)
+        with nc.allow_non_contiguous_dma(reason="two small vectors, one pair of channels a piece"):
+            nc.sync.dma_start(out=gain_bf[:], in_=norm1_w.rearrange("(a p e) -> p a e", p=P, e=2))
+            nc.sync.dma_start(out=beta_bf[:], in_=norm1_b.rearrange("(a p e) -> p a e", p=P, e=2))
+        bias_row = const.tile([P, 3 * C], BF16)
+        nc.vector.memset(bias_row[:], 0.0)
+        nc.sync.dma_start(out=bias_row[0:1, :], in_=qkv_b.rearrange("(o n) -> o n", o=1))
+
+        w_raw = [const.tile([P, ROW_TILES, C], BF16, name="w_raw%d" % n) for n in range(N_CHUNKS)]
+        for n in range(N_CHUNKS):
+            rows = qkv_w[N_COLS * n : N_COLS * (n + 1), :]
+            nc.sync.dma_start(out=w_raw[n][:], in_=rows.rearrange("(j p) k -> p j k", p=P))
+
+        gain = const.tile([P, 2 * QUARTERS], F32)
+        beta = const.tile([P, 2 * QUARTERS], F32)
+        nc.vector.tensor_copy(out=gain[:], in_=gain_bf[:].rearrange("p a e -> p (a e)"))
+        nc.vector.tensor_copy(out=beta[:], in_=beta_bf[:].rearrange("p a e -> p (a e)"))
+
+        ones = const.tile([P, P], BF16)
+        nc.vector.memset(ones[:], 1.0)
+        bias_all = const.tile([P, 3 * C], F32)
+        for n in range(N_CHUNKS):
+            cols = slice(N_COLS * n, N_COLS * (n + 1))
+            spread = acc_pool.tile([P, N_COLS], F32, tag="acc")
+            nc.tensor.matmul(out=spread[:], lhsT=ones[:], rhs=bias_row[:, cols], start=True, stop=True)
+            nc.scalar.copy(out=bias_all[:, cols], in_=spread[:])
+
+        eps = const.tile([P, 1], F32)
+        nc.vector.memset(eps[:], EPS)
+        warm = const.tile([P, 1], F32)
+        nc.scalar.activation(out=warm[:], in_=eps[:], func=ACT.Sqrt)
+
+        ident = const.tile([P, P], F32)
+        make_identity(nc, ident[:])
+        by_grid = ident[:].rearrange("p (b i h) -> p b h i", b=IMAGES, h=2)
+        roll_same = const.tile([P, P], F32)
+        same = roll_same[:].rearrange("p (b wi wj r) -> p b wi wj r", b=IMAGES, wi=2, wj=2)
+        wrap = GRID - WS - SHIFT
+        nc.vector.tensor_copy(out=same[:, :, 0, :, :], in_=by_grid[:, :, :, SHIFT : SHIFT + WS])
+        nc.vector.tensor_copy(out=same[:, :, 1, :, 0:wrap], in_=by_grid[:, :, :, SHIFT + WS : GRID])
+        nc.vector.tensor_copy(out=same[:, :, 1, :, wrap:WS], in_=by_grid[:, :, :, 0:SHIFT])
+        roll_swap = const.tile([P, P], F32)
+        swap = roll_swap[:].rearrange("p (b wi wj r) -> p b wi wj r", b=IMAGES, wi=2, wj=2)
+        nc.vector.tensor_copy(out=swap[:, :, :, 0, :], in_=same[:, :, :, 1, :])
+        nc.vector.tensor_copy(out=swap[:, :, :, 1, :], in_=same[:, :, :, 0, :])
+
+        x_codes = const.tile([P, WS // PAIR, PASSES, PAIR * P], U32, align_bytes=64)
+        x_scales = const.tile([P, WS // PAIR, PASSES, PAIR * P], U8, align_bytes=64)
+        w_codes = [
+            const.tile([P, PASSES, N_COLS], U32, name="w_codes%d" % n, align_bytes=64)
+            for n in range(N_CHUNKS)
+        ]
+        w_scales = [
+            const.tile([P, PASSES, N_COLS], U8, name="w_scales%d" % n, align_bytes=64)
+            for n in range(N_CHUNKS)
+        ]
+
+        def norm_pair(pair):
+            stats = small.tile([P, PAIR, 2, 6], F32)
+            mean_var = small.tile([P, PAIR, 2], F32)
+            for i in range(PAIR):
+                for half in range(2):
+                    nc.vector.bn_stats(
+                        out=stats[:, i, half, :],
+                        in_=x_raw[:, PAIR * pair + i, (C // 2) * half : (C // 2) * (half + 1)],
+                    )
+                nc.vector.bn_aggr(
+                    out=mean_var[:, i, :], in_=stats[:, i, :, :].rearrange("p h s -> p (h s)")
+                )
+            std = small.tile([P, PAIR], F32)
+            nc.scalar.activation(
+                out=std[:], in_=mean_var[:, :, 1], func=ACT.Sqrt, bias=eps[:, 0:1], scale=1.0
+            )
+            rstd = small.tile([P, PAIR], F32)
+            nc.vector.reciprocal(out=rstd[:], in_=std[:])
+            shift = small.tile([P, PAIR], F32)
+            nc.vector.scalar_tensor_tensor(
+                out=shift[:], in0=mean_var[:, :, 0], scalar=-1.0, in1=rstd[:], op0=ALU.mult, op1=ALU.mult
+            )
+            centred = work.tile([P, PAIR, C], F32)
+            for i in range(PAIR):
+                nc.gpsimd.tensor_scalar(
+                    out=centred[:, i, :].rearrange("p (a e k) -> p a e k", a=QUARTERS, e=2),
+                    in0=x_raw[:, PAIR * pair + i, :].rearrange("p (a k e) -> p a e k", a=QUARTERS, e=2),
+                    scalar1=rstd[:, i : i + 1],
+                    scalar2=shift[:, i : i + 1],
+                    op0=ALU.mult,
+                    op1=ALU.add,
+                )
+            planes = work.tile([P, 2 * QUARTERS, PAIR * P], BF16)
+            for a in range(QUARTERS):
+                flipped = flip_pool.tile([P, 2, PAIR, P], F32, tag="flip")
+                for e in range(2):
+                    for i in range(PAIR):
+                        block = 2 * a + e
+                        nc.tensor.transpose(
+                            out=flipped[:, e, i, :],
+                            in_=centred[:, i, P * block : P * (block + 1)],
+                            identity=(roll_same if PAIR * pair + i >= SHIFT else roll_swap)[:],
+                        )
+                for e in range(2):
+                    block = 2 * a + e
+                    nc.scalar.activation(
+                        out=planes[:, block, :],
+                        in_=flipped[:, e, :, :].rearrange("p i m -> p (i m)"),
+                        func=ACT.Identity,
+                        scale=gain[:, block : block + 1],
+                        bias=beta[:, block : block + 1],
+                    )
+            grouped = work.tile([P, PASSES, PAIR * P, PACK], BF16, align_bytes=64)
+            for g in range(PASSES):
+                nc.vector.tensor_copy(
+                    out=grouped[:, g, :, :],
+                    in_=planes[:, PACK * g : PACK * (g + 1), :].rearrange("p t m -> p m t"),
+                )
+            nc.vector.quantize_mx(
+                out=x_codes[:, pair, :, :].rearrange("p g m -> p (g m)").bitcast(FP8X4),
+                scales=x_scales[:, pair, :, :].rearrange("p g m -> p (g m)"),
+                in_=grouped[:].rearrange("p g m t -> p (g m t)"),
+            )
+
+        def quantise_weights(n):
+            words = w_raw[n][:].bitcast(F32)
+            w_grouped = work.tile([P, PASSES, N_COLS, PACK], BF16, align_bytes=64)
+            grouped_words = w_grouped[:].bitcast(F32)
+            for g in range(PASSES):
+                for half in range(2):
+                    flipped = flip_pool.tile([P, 2, 2 * P], F32, tag="flip")
+                    for u in range(2):
+                        for jj in range(2):
+                            a = 2 * g + u
+                            nc.tensor.transpose(
+                                out=flipped[:, u, P * jj : P * (jj + 1)],
+                                in_=words[:, 2 * half + jj, P * a : P * (a + 1)],
+                                identity=ident[:],
+                            )
+                    nc.scalar.copy(
+                        out=grouped_words[:, g, 2 * P * half : 2 * P * (half + 1), :],
+                        in_=flipped[:].rearrange("p u c -> p c u"),
+                    )
+            nc.vector.quantize_mx(
+                out=w_codes[n][:].rearrange("p g c -> p (g c)").bitcast(FP8X4),
+                scales=w_scales[n][:].rearrange("p g c -> p (g c)"),
+                in_=w_grouped[:].rearrange("p g c t -> p (g c t)"),
+            )
+
+        def project(n):
+            stage = stage_pool.tile([P, HEADS, WS, HD], F32)
+            bias_n = bias_all[:, N_COLS * n : N_COLS * (n + 1)].rearrange("p (a d) -> p a d", d=HD)
+            for e in range(WS):
+                c = (e - SHIFT) % WS
+                pair, i = divmod(e, PAIR)
+                tokens = slice(P * i, P * (i + 1))
+                acc = acc_pool.tile([P, N_COLS], F32, tag="acc")
+                for g in range(PASSES):
+                    nc.tensor.matmul_mx(
+                        out=acc[:],
+                        lhsT=x_codes[:, pair, g, tokens].bitcast(FP8X4),
+                        lhsT_scale=x_scales[:, pair, g, tokens],
+                        rhs=w_codes[n][:, g, :].bitcast(FP8X4),
+                        rhs_scale=w_scales[n][:, g, :],
+                        start=(g == 0),
+                        stop=(g == PASSES - 1),
+                    )
+                by_head = acc[:].rearrange("p (a d) -> p a d", d=HD)
+                if e % SCALAR_EVERY == 0:
+                    nc.scalar.copy(out=stage[:, :, c, :], in_=by_head)
+                    nc.gpsimd.tensor_tensor(
+                        out=stage[:, :, c, :], in0=stage[:, :, c, :], in1=bias_n, op=ALU.add
+                    )
+                else:
+                    nc.vector.tensor_tensor(out=stage[:, :, c, :], in0=by_head, in1=bias_n, op=ALU.add)
+            rows_of = outs[n // 2].rearrange("w a (r c) d -> a w r (c d)", c=WS)
+            for a in range(HEADS):
+                nc.sync.dma_start(
+                    out=rows_of[HEADS * (n % 2) + a],
+                    in_=stage[:, a, :, :].rearrange("p c d -> p (c d)"),
+                )
+
+        norm_pair(0)
+        norm_pair(1)
+        quantise_weights(0)
+        norm_pair(2)
+        norm_pair(3)
+        quantise_weights(1)
+        for n in range(N_CHUNKS):
+            if n + 2 < N_CHUNKS:
+                quantise_weights(n + 2)
+            project(n)

@@ -19,12 +19,17 @@ HD = 32
 PACK = 4
 PASSES = C // (P * PACK)
 QUARTERS = C // (2 * P)
-N_COLS = 512
-N_CHUNKS = 3 * C // N_COLS
-HEADS = N_COLS // HD
-ROW_TILES = N_COLS // P
+PLANES = C // P
 PAIR = 2
-SCALAR_EVERY = 4
+N_PAIRS = WS // PAIR
+W_ROWS = 512
+N_CHUNKS = 3 * C // W_ROWS
+ROW_TILES = W_ROWS // P
+N_COLS = 256
+HEADS = N_COLS // HD
+BANKS = 8
+FLIP_LAG = 3
+SCALE_LAG = 4
 
 FLOPS = 2 * IMAGES * GRID * GRID * C * 3 * C
 
@@ -36,46 +41,45 @@ def tile_swintransformerblock_pa_kernel(
     outs = (out_0, out_1, out_2)
 
     with ExitStack() as ctx:
+        ctx.enter_context(tc.manual_schedule())
         const = ctx.enter_context(tc.tile_pool(name="const", bufs=1))
         small = ctx.enter_context(tc.tile_pool(name="small", bufs=4))
+        centred_pool = ctx.enter_context(tc.tile_pool(name="centred", bufs=3))
         work = ctx.enter_context(tc.tile_pool(name="work", bufs=2))
-        stage_pool = ctx.enter_context(tc.tile_pool(name="stage", bufs=3))
-        flip_pool = ctx.enter_context(tc.psum_pool(name="flip", bufs=4))
-        acc_pool = ctx.enter_context(tc.psum_pool(name="acc", bufs=4))
+        stage_pool = ctx.enter_context(tc.tile_pool(name="stage", bufs=4))
+        psum = ctx.enter_context(tc.psum_pool(name="psum", bufs=BANKS))
 
         x_raw = const.tile([P, WS, C], BF16)
         x_rows = x.rearrange("b (q e) k -> (b q) e k", e=WS)
-        for pair in range(WS // PAIR):
-            tiles = slice(PAIR * pair, PAIR * (pair + 1))
-            nc.sync.dma_start(out=x_raw[:, tiles, :], in_=x_rows[:, tiles, :])
+        w_raw = [const.tile([P, ROW_TILES, C], BF16, name="w_raw%d" % n) for n in range(N_CHUNKS)]
+        bias_all = const.tile([P, 3 * C], BF16)
+
+        def tile_of(c):
+            return (c + SHIFT) % WS
+
+        def load_tokens(first, last):
+            nc.sync.dma_start(out=x_raw[:, first:last, :], in_=x_rows[:, first:last, :])
+
+        def load_weights(n):
+            rows = qkv_w[W_ROWS * n : W_ROWS * (n + 1), :]
+            nc.sync.dma_start(out=w_raw[n][:], in_=rows.rearrange("(j p) k -> p j k", p=P))
+
+        load_tokens(SHIFT, SHIFT + PAIR)
+        load_tokens(SHIFT + PAIR, WS)
+        load_weights(0)
+        load_tokens(0, SHIFT)
+        load_weights(1)
+        nc.sync.dma_start(out=bias_all[:], in_=qkv_b.partition_broadcast(P))
+        for n in range(2, N_CHUNKS):
+            load_weights(n)
 
         gain_bf = const.tile([P, QUARTERS, 2], BF16)
         beta_bf = const.tile([P, QUARTERS, 2], BF16)
         with nc.allow_non_contiguous_dma(reason="two small vectors, one pair of channels a piece"):
-            nc.sync.dma_start(out=gain_bf[:], in_=norm1_w.rearrange("(a p e) -> p a e", p=P, e=2))
-            nc.sync.dma_start(out=beta_bf[:], in_=norm1_b.rearrange("(a p e) -> p a e", p=P, e=2))
-        bias_row = const.tile([P, 3 * C], BF16)
-        nc.vector.memset(bias_row[:], 0.0)
-        nc.sync.dma_start(out=bias_row[0:1, :], in_=qkv_b.rearrange("(o n) -> o n", o=1))
-
-        w_raw = [const.tile([P, ROW_TILES, C], BF16, name="w_raw%d" % n) for n in range(N_CHUNKS)]
-        for n in range(N_CHUNKS):
-            rows = qkv_w[N_COLS * n : N_COLS * (n + 1), :]
-            nc.sync.dma_start(out=w_raw[n][:], in_=rows.rearrange("(j p) k -> p j k", p=P))
-
-        gain = const.tile([P, 2 * QUARTERS], F32)
-        beta = const.tile([P, 2 * QUARTERS], F32)
-        nc.vector.tensor_copy(out=gain[:], in_=gain_bf[:].rearrange("p a e -> p (a e)"))
-        nc.vector.tensor_copy(out=beta[:], in_=beta_bf[:].rearrange("p a e -> p (a e)"))
-
-        ones = const.tile([P, P], BF16)
-        nc.vector.memset(ones[:], 1.0)
-        bias_all = const.tile([P, 3 * C], F32)
-        for n in range(N_CHUNKS):
-            cols = slice(N_COLS * n, N_COLS * (n + 1))
-            spread = acc_pool.tile([P, N_COLS], F32, tag="acc")
-            nc.tensor.matmul(out=spread[:], lhsT=ones[:], rhs=bias_row[:, cols], start=True, stop=True)
-            nc.scalar.copy(out=bias_all[:, cols], in_=spread[:])
+            nc.scalar.dma_start(out=gain_bf[:], in_=norm1_w.rearrange("(a p e) -> p a e", p=P, e=2))
+            nc.scalar.dma_start(out=beta_bf[:], in_=norm1_b.rearrange("(a p e) -> p a e", p=P, e=2))
+        gain = const.tile([P, PLANES], F32)
+        beta = const.tile([P, PLANES], F32)
 
         eps = const.tile([P, 1], F32)
         nc.vector.memset(eps[:], EPS)
@@ -96,146 +100,187 @@ def tile_swintransformerblock_pa_kernel(
         nc.vector.tensor_copy(out=swap[:, :, :, 0, :], in_=same[:, :, :, 1, :])
         nc.vector.tensor_copy(out=swap[:, :, :, 1, :], in_=same[:, :, :, 0, :])
 
-        x_codes = const.tile([P, WS // PAIR, PASSES, PAIR * P], U32, align_bytes=64)
-        x_scales = const.tile([P, WS // PAIR, PASSES, PAIR * P], U8, align_bytes=64)
+        x_codes = const.tile([P, N_PAIRS, PASSES, PAIR * P], U32, align_bytes=64)
+        x_scales = const.tile([P, N_PAIRS, PASSES, PAIR * P], U8, align_bytes=64)
         w_codes = [
-            const.tile([P, PASSES, N_COLS], U32, name="w_codes%d" % n, align_bytes=64)
+            const.tile([P, PASSES, W_ROWS], U32, name="w_codes%d" % n, align_bytes=64)
             for n in range(N_CHUNKS)
         ]
         w_scales = [
-            const.tile([P, PASSES, N_COLS], U8, name="w_scales%d" % n, align_bytes=64)
+            const.tile([P, PASSES, W_ROWS], U8, name="w_scales%d" % n, align_bytes=64)
             for n in range(N_CHUNKS)
         ]
+        mean_var = const.tile([P, WS, 2], F32)
+        std = const.tile([P, WS], F32)
+        neg_mean = const.tile([P, WS], F32)
+        rstd = const.tile([P, WS], F32)
+        planes = [const.tile([P, PLANES, PAIR * P], BF16, name="planes%d" % q) for q in range(N_PAIRS)]
+        centred = {}
+        flipped = {}
+        grouped = {}
+        w_grouped = {}
 
-        def norm_pair(pair):
-            stats = small.tile([P, PAIR, 2, 6], F32)
-            mean_var = small.tile([P, PAIR, 2], F32)
-            for i in range(PAIR):
-                for half in range(2):
-                    nc.vector.bn_stats(
-                        out=stats[:, i, half, :],
-                        in_=x_raw[:, PAIR * pair + i, (C // 2) * half : (C // 2) * (half + 1)],
-                    )
-                nc.vector.bn_aggr(
-                    out=mean_var[:, i, :], in_=stats[:, i, :, :].rearrange("p h s -> p (h s)")
+        def statistics(c):
+            stats = small.tile([P, 2, 6], F32)
+            for half in range(2):
+                nc.vector.bn_stats(
+                    out=stats[:, half, :],
+                    in_=x_raw[:, tile_of(c), (C // 2) * half : (C // 2) * (half + 1)],
                 )
-            std = small.tile([P, PAIR], F32)
+            nc.vector.bn_aggr(out=mean_var[:, c, :], in_=stats[:].rearrange("p h s -> p (h s)"))
             nc.scalar.activation(
-                out=std[:], in_=mean_var[:, :, 1], func=ACT.Sqrt, bias=eps[:, 0:1], scale=1.0
+                out=std[:, c : c + 1], in_=mean_var[:, c, 1:2], func=ACT.Sqrt, bias=eps[:, 0:1], scale=1.0
             )
-            rstd = small.tile([P, PAIR], F32)
-            nc.vector.reciprocal(out=rstd[:], in_=std[:])
-            shift = small.tile([P, PAIR], F32)
-            nc.vector.scalar_tensor_tensor(
-                out=shift[:], in0=mean_var[:, :, 0], scalar=-1.0, in1=rstd[:], op0=ALU.mult, op1=ALU.mult
-            )
-            centred = work.tile([P, PAIR, C], F32)
-            for i in range(PAIR):
-                nc.gpsimd.tensor_scalar(
-                    out=centred[:, i, :].rearrange("p (a e k) -> p a e k", a=QUARTERS, e=2),
-                    in0=x_raw[:, PAIR * pair + i, :].rearrange("p (a k e) -> p a e k", a=QUARTERS, e=2),
-                    scalar1=rstd[:, i : i + 1],
-                    scalar2=shift[:, i : i + 1],
-                    op0=ALU.mult,
-                    op1=ALU.add,
-                )
-            planes = work.tile([P, 2 * QUARTERS, PAIR * P], BF16)
-            for a in range(QUARTERS):
-                flipped = flip_pool.tile([P, 2, PAIR, P], F32, tag="flip")
-                for e in range(2):
-                    for i in range(PAIR):
-                        block = 2 * a + e
-                        nc.tensor.transpose(
-                            out=flipped[:, e, i, :],
-                            in_=centred[:, i, P * block : P * (block + 1)],
-                            identity=(roll_same if PAIR * pair + i >= SHIFT else roll_swap)[:],
-                        )
-                for e in range(2):
-                    block = 2 * a + e
-                    nc.scalar.activation(
-                        out=planes[:, block, :],
-                        in_=flipped[:, e, :, :].rearrange("p i m -> p (i m)"),
-                        func=ACT.Identity,
-                        scale=gain[:, block : block + 1],
-                        bias=beta[:, block : block + 1],
-                    )
-            grouped = work.tile([P, PASSES, PAIR * P, PACK], BF16, align_bytes=64)
-            for g in range(PASSES):
-                nc.vector.tensor_copy(
-                    out=grouped[:, g, :, :],
-                    in_=planes[:, PACK * g : PACK * (g + 1), :].rearrange("p t m -> p m t"),
-                )
-            nc.vector.quantize_mx(
-                out=x_codes[:, pair, :, :].rearrange("p g m -> p (g m)").bitcast(FP8X4),
-                scales=x_scales[:, pair, :, :].rearrange("p g m -> p (g m)"),
-                in_=grouped[:].rearrange("p g m t -> p (g m t)"),
+            nc.scalar.activation(
+                out=neg_mean[:, c : c + 1], in_=mean_var[:, c, 0:1], func=ACT.Identity, scale=-1.0
             )
 
-        def quantise_weights(n):
+        def centre(c):
+            nc.vector.reciprocal(out=rstd[:, c : c + 1], in_=std[:, c : c + 1])
+            q, i = divmod(c, PAIR)
+            if i == 0:
+                centred[q] = centred_pool.tile([P, PAIR, C], F32, name="centred")
+            nc.gpsimd.tensor_scalar(
+                out=centred[q][:, i, :].rearrange("p (a e k) -> p a e k", a=QUARTERS, e=2),
+                in0=x_raw[:, tile_of(c), :].rearrange("p (a k e) -> p a e k", a=QUARTERS, e=2),
+                scalar1=neg_mean[:, c : c + 1],
+                scalar2=rstd[:, c : c + 1],
+                op0=ALU.add,
+                op1=ALU.mult,
+            )
+
+        def flip_tokens(q, g):
+            flipped[q, g] = []
+            for u in range(2):
+                bank = psum.tile([P, 2, PAIR, P], F32, tag="bank", name="flipped")
+                for e in range(2):
+                    plane = PACK * g + 2 * u + e
+                    for i in range(PAIR):
+                        nc.tensor.transpose(
+                            out=bank[:, e, i, :],
+                            in_=centred[q][:, i, P * plane : P * (plane + 1)],
+                            identity=(roll_same if PAIR * q + i < WS - SHIFT else roll_swap)[:],
+                        )
+                flipped[q, g].append(bank)
+
+        def scale_tokens(q, g):
+            for u in range(2):
+                for e in range(2):
+                    plane = PACK * g + 2 * u + e
+                    nc.scalar.activation(
+                        out=planes[q][:, plane, :],
+                        in_=flipped[q, g][u][:, e, :, :].rearrange("p i m -> p (i m)"),
+                        func=ACT.Identity,
+                        scale=gain[:, plane : plane + 1],
+                        bias=beta[:, plane : plane + 1],
+                    )
+
+        def regroup_tokens(q, g):
+            if g == 0:
+                grouped[q] = work.tile([P, PASSES, PAIR * P, PACK], BF16, name="grouped", align_bytes=64)
+            nc.vector.tensor_copy(
+                out=grouped[q][:, g, :, :].rearrange("p (m i) t -> p m t i", i=4),
+                in_=planes[q][:, PACK * g : PACK * (g + 1), :].rearrange("p t (m i) -> p m t i", i=4),
+            )
+
+        def quantise_tokens(q):
+            nc.vector.quantize_mx(
+                out=x_codes[:, q, :, :].rearrange("p g m -> p (g m)").bitcast(FP8X4),
+                scales=x_scales[:, q, :, :].rearrange("p g m -> p (g m)"),
+                in_=grouped[q][:].rearrange("p g m t -> p (g m t)"),
+            )
+
+        def flip_weights(n):
             words = w_raw[n][:].bitcast(F32)
-            w_grouped = work.tile([P, PASSES, N_COLS, PACK], BF16, align_bytes=64)
-            grouped_words = w_grouped[:].bitcast(F32)
+            w_grouped[n] = work.tile([P, PASSES, W_ROWS, PACK], BF16, name="w_grouped", align_bytes=64)
+            grouped_words = w_grouped[n][:].bitcast(F32)
             for g in range(PASSES):
                 for half in range(2):
-                    flipped = flip_pool.tile([P, 2, 2 * P], F32, tag="flip")
+                    bank = psum.tile([P, 2, 2 * P], F32, tag="bank", name="w_flipped")
                     for u in range(2):
                         for jj in range(2):
                             a = 2 * g + u
                             nc.tensor.transpose(
-                                out=flipped[:, u, P * jj : P * (jj + 1)],
+                                out=bank[:, u, P * jj : P * (jj + 1)],
                                 in_=words[:, 2 * half + jj, P * a : P * (a + 1)],
                                 identity=ident[:],
                             )
                     nc.scalar.copy(
                         out=grouped_words[:, g, 2 * P * half : 2 * P * (half + 1), :],
-                        in_=flipped[:].rearrange("p u c -> p c u"),
+                        in_=bank[:].rearrange("p u c -> p c u"),
                     )
+
+        def quantise_weights(n):
             nc.vector.quantize_mx(
                 out=w_codes[n][:].rearrange("p g c -> p (g c)").bitcast(FP8X4),
                 scales=w_scales[n][:].rearrange("p g c -> p (g c)"),
-                in_=w_grouped[:].rearrange("p g c t -> p (g c t)"),
+                in_=w_grouped[n][:].rearrange("p g c t -> p (g c t)"),
             )
 
-        def project(n):
+        def project(n, half):
             stage = stage_pool.tile([P, HEADS, WS, HD], F32)
-            bias_n = bias_all[:, N_COLS * n : N_COLS * (n + 1)].rearrange("p (a d) -> p a d", d=HD)
-            for e in range(WS):
-                c = (e - SHIFT) % WS
-                pair, i = divmod(e, PAIR)
-                tokens = slice(P * i, P * (i + 1))
-                acc = acc_pool.tile([P, N_COLS], F32, tag="acc")
-                for g in range(PASSES):
-                    nc.tensor.matmul_mx(
-                        out=acc[:],
-                        lhsT=x_codes[:, pair, g, tokens].bitcast(FP8X4),
-                        lhsT_scale=x_scales[:, pair, g, tokens],
-                        rhs=w_codes[n][:, g, :].bitcast(FP8X4),
-                        rhs_scale=w_scales[n][:, g, :],
-                        start=(g == 0),
-                        stop=(g == PASSES - 1),
-                    )
-                by_head = acc[:].rearrange("p (a d) -> p a d", d=HD)
-                if e % SCALAR_EVERY == 0:
-                    nc.scalar.copy(out=stage[:, :, c, :], in_=by_head)
-                    nc.gpsimd.tensor_tensor(
-                        out=stage[:, :, c, :], in0=stage[:, :, c, :], in1=bias_n, op=ALU.add
-                    )
+            cols = slice(N_COLS * half, N_COLS * (half + 1))
+            first_col = W_ROWS * n + N_COLS * half
+            bias = (
+                bias_all[:, first_col : first_col + N_COLS]
+                .rearrange("p (a d) -> p a d", d=HD)
+                .unsqueeze(2)
+                .to_broadcast([P, HEADS, PAIR, HD])
+            )
+            for q in range(N_PAIRS):
+                acc = psum.tile([P, PAIR, N_COLS], F32, tag="bank")
+                for i in range(PAIR):
+                    tokens = slice(P * i, P * (i + 1))
+                    for g in range(PASSES):
+                        nc.tensor.matmul_mx(
+                            out=acc[:, i, :],
+                            lhsT=x_codes[:, q, g, tokens].bitcast(FP8X4),
+                            lhsT_scale=x_scales[:, q, g, tokens],
+                            rhs=w_codes[n][:, g, cols].bitcast(FP8X4),
+                            rhs_scale=w_scales[n][:, g, cols],
+                            start=(g == 0),
+                            stop=(g == PASSES - 1),
+                        )
+                by_head = acc[:].rearrange("p i (a d) -> p a i d", d=HD)
+                place = stage[:, :, PAIR * q : PAIR * (q + 1), :]
+                if q < PAIR - half:
+                    nc.scalar.copy(out=place, in_=by_head)
+                    nc.gpsimd.tensor_tensor(out=place, in0=place, in1=bias, op=ALU.add)
                 else:
-                    nc.vector.tensor_tensor(out=stage[:, :, c, :], in0=by_head, in1=bias_n, op=ALU.add)
+                    nc.vector.tensor_tensor(out=place, in0=by_head, in1=bias, op=ALU.add)
             rows_of = outs[n // 2].rearrange("w a (r c) d -> a w r (c d)", c=WS)
+            first_head = (first_col % C) // HD
             for a in range(HEADS):
                 nc.sync.dma_start(
-                    out=rows_of[HEADS * (n % 2) + a],
-                    in_=stage[:, a, :, :].rearrange("p c d -> p (c d)"),
+                    out=rows_of[first_head + a], in_=stage[:, a, :, :].rearrange("p c d -> p (c d)")
                 )
 
-        norm_pair(0)
-        norm_pair(1)
+        for step in range(WS + SCALE_LAG):
+            if step < WS:
+                statistics(step)
+            if 1 <= step <= WS:
+                centre(step - 1)
+            if step == FLIP_LAG:
+                nc.vector.tensor_copy(out=gain[:], in_=gain_bf[:].rearrange("p a e -> p (a e)"))
+                nc.vector.tensor_copy(out=beta[:], in_=beta_bf[:].rearrange("p a e -> p (a e)"))
+                flip_weights(0)
+            if 0 <= step - FLIP_LAG < WS:
+                flip_tokens(*divmod(step - FLIP_LAG, PASSES))
+            if 0 <= step - SCALE_LAG < WS:
+                scale_tokens(*divmod(step - SCALE_LAG, PASSES))
+        flip_weights(1)
         quantise_weights(0)
-        norm_pair(2)
-        norm_pair(3)
-        quantise_weights(1)
+        for q in range(N_PAIRS):
+            for g in range(PASSES):
+                regroup_tokens(q, g)
+            if q > 0:
+                quantise_tokens(q - 1)
+        quantise_tokens(N_PAIRS - 1)
+
         for n in range(N_CHUNKS):
+            project(n, 0)
+            if n + 1 < N_CHUNKS:
+                quantise_weights(n + 1)
             if n + 2 < N_CHUNKS:
-                quantise_weights(n + 2)
-            project(n)
+                flip_weights(n + 2)
+            project(n, 1)

@@ -20,6 +20,8 @@ PACK = 4
 PASSES = C // (P * PACK)
 QUARTERS = C // (2 * P)
 PLANES = C // P
+QUAD = 4
+N_QUADS = WS // QUAD
 PAIR = 2
 N_PAIRS = WS // PAIR
 W_ROWS = 512
@@ -28,8 +30,7 @@ ROW_TILES = W_ROWS // P
 N_COLS = 256
 HEADS = N_COLS // HD
 BANKS = 8
-FLIP_LAG = 3
-SCALE_LAG = 4
+FLIP_LAG = QUAD + 1
 
 FLOPS = 2 * IMAGES * GRID * GRID * C * 3 * C
 
@@ -44,7 +45,6 @@ def tile_swintransformerblock_pa_kernel(
         ctx.enter_context(tc.manual_schedule())
         const = ctx.enter_context(tc.tile_pool(name="const", bufs=1))
         small = ctx.enter_context(tc.tile_pool(name="small", bufs=4))
-        centred_pool = ctx.enter_context(tc.tile_pool(name="centred", bufs=3))
         work = ctx.enter_context(tc.tile_pool(name="work", bufs=2))
         stage_pool = ctx.enter_context(tc.tile_pool(name="stage", bufs=4))
         psum = ctx.enter_context(tc.psum_pool(name="psum", bufs=BANKS))
@@ -67,8 +67,8 @@ def tile_swintransformerblock_pa_kernel(
         load_tokens(SHIFT, SHIFT + PAIR)
         load_tokens(SHIFT + PAIR, WS)
         load_weights(0)
-        load_tokens(0, SHIFT)
         load_weights(1)
+        load_tokens(0, SHIFT)
         nc.sync.dma_start(out=bias_all[:], in_=qkv_b.partition_broadcast(P))
         for n in range(2, N_CHUNKS):
             load_weights(n)
@@ -100,8 +100,8 @@ def tile_swintransformerblock_pa_kernel(
         nc.vector.tensor_copy(out=swap[:, :, :, 0, :], in_=same[:, :, :, 1, :])
         nc.vector.tensor_copy(out=swap[:, :, :, 1, :], in_=same[:, :, :, 0, :])
 
-        x_codes = const.tile([P, N_PAIRS, PASSES, PAIR * P], U32, align_bytes=64)
-        x_scales = const.tile([P, N_PAIRS, PASSES, PAIR * P], U8, align_bytes=64)
+        x_codes = const.tile([P, N_QUADS, PASSES, QUAD * P], U32, align_bytes=64)
+        x_scales = const.tile([P, N_QUADS, PASSES, QUAD * P], U8, align_bytes=64)
         w_codes = [
             const.tile([P, PASSES, W_ROWS], U32, name="w_codes%d" % n, align_bytes=64)
             for n in range(N_CHUNKS)
@@ -114,9 +114,8 @@ def tile_swintransformerblock_pa_kernel(
         std = const.tile([P, WS], F32)
         neg_mean = const.tile([P, WS], F32)
         rstd = const.tile([P, WS], F32)
-        planes = [const.tile([P, PLANES, PAIR * P], BF16, name="planes%d" % q) for q in range(N_PAIRS)]
+        planes = [const.tile([P, PLANES, QUAD * P], BF16, name="planes%d" % h) for h in range(N_QUADS)]
         centred = {}
-        flipped = {}
         grouped = {}
         w_grouped = {}
 
@@ -137,11 +136,11 @@ def tile_swintransformerblock_pa_kernel(
 
         def centre(c):
             nc.vector.reciprocal(out=rstd[:, c : c + 1], in_=std[:, c : c + 1])
-            q, i = divmod(c, PAIR)
+            h, i = divmod(c, QUAD)
             if i == 0:
-                centred[q] = centred_pool.tile([P, PAIR, C], F32, name="centred")
+                centred[h] = work.tile([P, QUAD, C], F32, name="centred")
             nc.gpsimd.tensor_scalar(
-                out=centred[q][:, i, :].rearrange("p (a e k) -> p a e k", a=QUARTERS, e=2),
+                out=centred[h][:, i, :].rearrange("p (a e k) -> p a e k", a=QUARTERS, e=2),
                 in0=x_raw[:, tile_of(c), :].rearrange("p (a k e) -> p a e k", a=QUARTERS, e=2),
                 scalar1=neg_mean[:, c : c + 1],
                 scalar2=rstd[:, c : c + 1],
@@ -149,45 +148,37 @@ def tile_swintransformerblock_pa_kernel(
                 op1=ALU.mult,
             )
 
-        def flip_tokens(q, g):
-            flipped[q, g] = []
-            for u in range(2):
-                bank = psum.tile([P, 2, PAIR, P], F32, tag="bank", name="flipped")
-                for e in range(2):
-                    plane = PACK * g + 2 * u + e
-                    for i in range(PAIR):
-                        nc.tensor.transpose(
-                            out=bank[:, e, i, :],
-                            in_=centred[q][:, i, P * plane : P * (plane + 1)],
-                            identity=(roll_same if PAIR * q + i < WS - SHIFT else roll_swap)[:],
-                        )
-                flipped[q, g].append(bank)
-
-        def scale_tokens(q, g):
-            for u in range(2):
-                for e in range(2):
-                    plane = PACK * g + 2 * u + e
-                    nc.scalar.activation(
-                        out=planes[q][:, plane, :],
-                        in_=flipped[q, g][u][:, e, :, :].rearrange("p i m -> p (i m)"),
-                        func=ACT.Identity,
-                        scale=gain[:, plane : plane + 1],
-                        bias=beta[:, plane : plane + 1],
+        def flip_tokens(h, a):
+            for e in range(2):
+                plane = 2 * a + e
+                bank = psum.tile([P, QUAD, P], F32, tag="bank", name="flipped")
+                for i in range(QUAD):
+                    nc.tensor.transpose(
+                        out=bank[:, i, :],
+                        in_=centred[h][:, i, P * plane : P * (plane + 1)],
+                        identity=(roll_same if QUAD * h + i < WS - SHIFT else roll_swap)[:],
                     )
+                nc.scalar.activation(
+                    out=planes[h][:, plane, :],
+                    in_=bank[:].rearrange("p i m -> p (i m)"),
+                    func=ACT.Identity,
+                    scale=gain[:, plane : plane + 1],
+                    bias=beta[:, plane : plane + 1],
+                )
 
-        def regroup_tokens(q, g):
+        def regroup_tokens(h, g):
             if g == 0:
-                grouped[q] = work.tile([P, PASSES, PAIR * P, PACK], BF16, name="grouped", align_bytes=64)
+                grouped[h] = work.tile([P, PASSES, QUAD * P, PACK], BF16, name="grouped", align_bytes=64)
             nc.vector.tensor_copy(
-                out=grouped[q][:, g, :, :].rearrange("p (m i) t -> p m t i", i=4),
-                in_=planes[q][:, PACK * g : PACK * (g + 1), :].rearrange("p t (m i) -> p m t i", i=4),
+                out=grouped[h][:, g, :, :].rearrange("p (m i) t -> p m t i", i=4),
+                in_=planes[h][:, PACK * g : PACK * (g + 1), :].rearrange("p t (m i) -> p m t i", i=4),
             )
 
-        def quantise_tokens(q):
+        def quantise_tokens(h, g):
             nc.vector.quantize_mx(
-                out=x_codes[:, q, :, :].rearrange("p g m -> p (g m)").bitcast(FP8X4),
-                scales=x_scales[:, q, :, :].rearrange("p g m -> p (g m)"),
-                in_=grouped[q][:].rearrange("p g m t -> p (g m t)"),
+                out=x_codes[:, h, g, :].bitcast(FP8X4),
+                scales=x_scales[:, h, g, :],
+                in_=grouped[h][:, g, :, :].rearrange("p m t -> p (m t)"),
             )
 
         def flip_weights(n):
@@ -230,12 +221,13 @@ def tile_swintransformerblock_pa_kernel(
             for q in range(N_PAIRS):
                 acc = psum.tile([P, PAIR, N_COLS], F32, tag="bank")
                 for i in range(PAIR):
-                    tokens = slice(P * i, P * (i + 1))
+                    h, tile_in_quad = divmod(PAIR * q + i, QUAD)
+                    tokens = slice(P * tile_in_quad, P * (tile_in_quad + 1))
                     for g in range(PASSES):
                         nc.tensor.matmul_mx(
                             out=acc[:, i, :],
-                            lhsT=x_codes[:, q, g, tokens].bitcast(FP8X4),
-                            lhsT_scale=x_scales[:, q, g, tokens],
+                            lhsT=x_codes[:, h, g, tokens].bitcast(FP8X4),
+                            lhsT_scale=x_scales[:, h, g, tokens],
                             rhs=w_codes[n][:, g, cols].bitcast(FP8X4),
                             rhs_scale=w_scales[n][:, g, cols],
                             start=(g == 0),
@@ -255,32 +247,30 @@ def tile_swintransformerblock_pa_kernel(
                     out=rows_of[first_head + a], in_=stage[:, a, :, :].rearrange("p c d -> p (c d)")
                 )
 
-        for step in range(WS + SCALE_LAG):
+        for step in range(WS + FLIP_LAG):
             if step < WS:
                 statistics(step)
             if 1 <= step <= WS:
                 centre(step - 1)
-            if step == FLIP_LAG:
+            if step == FLIP_LAG - 2:
+                flip_weights(0)
+            if step == FLIP_LAG - 1:
+                flip_weights(1)
                 nc.vector.tensor_copy(out=gain[:], in_=gain_bf[:].rearrange("p a e -> p (a e)"))
                 nc.vector.tensor_copy(out=beta[:], in_=beta_bf[:].rearrange("p a e -> p (a e)"))
-                flip_weights(0)
-            if 0 <= step - FLIP_LAG < WS:
-                flip_tokens(*divmod(step - FLIP_LAG, PASSES))
-            if 0 <= step - SCALE_LAG < WS:
-                scale_tokens(*divmod(step - SCALE_LAG, PASSES))
-        flip_weights(1)
+            if step >= FLIP_LAG:
+                flip_tokens(*divmod(step - FLIP_LAG, QUARTERS))
         quantise_weights(0)
-        for q in range(N_PAIRS):
+        quantise_weights(1)
+        for h in range(N_QUADS):
             for g in range(PASSES):
-                regroup_tokens(q, g)
-            if q > 0:
-                quantise_tokens(q - 1)
-        quantise_tokens(N_PAIRS - 1)
+                regroup_tokens(h, g)
+                quantise_tokens(h, g)
 
         for n in range(N_CHUNKS):
             project(n, 0)
-            if n + 1 < N_CHUNKS:
-                quantise_weights(n + 1)
             if n + 2 < N_CHUNKS:
                 flip_weights(n + 2)
             project(n, 1)
+            if n + 2 < N_CHUNKS:
+                quantise_weights(n + 2)

@@ -20,17 +20,15 @@ PACK = 4
 PASSES = C // (P * PACK)
 QUARTERS = C // (2 * P)
 PLANES = C // P
-QUAD = 4
-N_QUADS = WS // QUAD
 PAIR = 2
 N_PAIRS = WS // PAIR
-W_ROWS = 512
-N_CHUNKS = 3 * C // W_ROWS
-ROW_TILES = W_ROWS // P
 N_COLS = 256
+N_SLABS = 3 * C // N_COLS
+ROW_TILES = N_COLS // P
 HEADS = N_COLS // HD
 BANKS = 8
-FLIP_LAG = QUAD + 1
+FLIP_LAG = 3
+SCALE_LAG = 4
 
 FLOPS = 2 * IMAGES * GRID * GRID * C * 3 * C
 
@@ -45,14 +43,18 @@ def tile_swintransformerblock_pa_kernel(
         ctx.enter_context(tc.manual_schedule())
         const = ctx.enter_context(tc.tile_pool(name="const", bufs=1))
         small = ctx.enter_context(tc.tile_pool(name="small", bufs=4))
+        centred_pool = ctx.enter_context(tc.tile_pool(name="centred", bufs=3))
         work = ctx.enter_context(tc.tile_pool(name="work", bufs=2))
+        slab_pool = ctx.enter_context(tc.tile_pool(name="slab", bufs=4))
         stage_pool = ctx.enter_context(tc.tile_pool(name="stage", bufs=4))
         psum = ctx.enter_context(tc.psum_pool(name="psum", bufs=BANKS))
 
         x_raw = const.tile([P, WS, C], BF16)
         x_rows = x.rearrange("b (q e) k -> (b q) e k", e=WS)
-        w_raw = [const.tile([P, ROW_TILES, C], BF16, name="w_raw%d" % n) for n in range(N_CHUNKS)]
-        bias_all = const.tile([P, 3 * C], BF16)
+        w_raw = [const.tile([P, ROW_TILES, C], BF16, name="w_raw%d" % s) for s in range(N_SLABS)]
+        bias_row = const.tile([P, 3 * C], BF16)
+        nc.gpsimd.memset(bias_row[:].bitcast(F32), 0.0)
+        bias_all = const.tile([P, 3 * C], F32)
 
         def tile_of(c):
             return (c + SHIFT) % WS
@@ -60,31 +62,33 @@ def tile_swintransformerblock_pa_kernel(
         def load_tokens(first, last):
             nc.sync.dma_start(out=x_raw[:, first:last, :], in_=x_rows[:, first:last, :])
 
-        def load_weights(n):
-            rows = qkv_w[W_ROWS * n : W_ROWS * (n + 1), :]
-            nc.sync.dma_start(out=w_raw[n][:], in_=rows.rearrange("(j p) k -> p j k", p=P))
+        def load_weights(s):
+            rows = qkv_w[N_COLS * s : N_COLS * (s + 1), :]
+            nc.sync.dma_start(out=w_raw[s][:], in_=rows.rearrange("(j p) k -> p j k", p=P))
 
-        load_tokens(SHIFT, SHIFT + PAIR)
-        load_tokens(SHIFT + PAIR, WS)
+        load_tokens(SHIFT, SHIFT + 1)
+        load_tokens(SHIFT + 1, SHIFT + 3)
         load_weights(0)
+        load_tokens(SHIFT + 3, WS)
         load_weights(1)
         load_tokens(0, SHIFT)
-        nc.sync.dma_start(out=bias_all[:], in_=qkv_b.partition_broadcast(P))
-        for n in range(2, N_CHUNKS):
-            load_weights(n)
+        for s in range(2, N_SLABS):
+            load_weights(s)
 
         gain_bf = const.tile([P, QUARTERS, 2], BF16)
         beta_bf = const.tile([P, QUARTERS, 2], BF16)
         with nc.allow_non_contiguous_dma(reason="two small vectors, one pair of channels a piece"):
             nc.scalar.dma_start(out=gain_bf[:], in_=norm1_w.rearrange("(a p e) -> p a e", p=P, e=2))
             nc.scalar.dma_start(out=beta_bf[:], in_=norm1_b.rearrange("(a p e) -> p a e", p=P, e=2))
+        nc.scalar.dma_start(out=bias_row[0:1, :], in_=qkv_b.rearrange("(o n) -> o n", o=1))
         gain = const.tile([P, PLANES], F32)
         beta = const.tile([P, PLANES], F32)
 
-        eps = const.tile([P, 1], F32)
-        nc.vector.memset(eps[:], EPS)
-        warm = const.tile([P, 1], F32)
-        nc.scalar.activation(out=warm[:], in_=eps[:], func=ACT.Sqrt)
+        warm = const.tile([P, 2], F32)
+        nc.vector.memset(warm[:, 0:1], 1.0)
+        nc.scalar.activation(out=warm[:, 1:2], in_=warm[:, 0:1], func=ACT.Sqrt)
+        ones = const.tile([P, P], BF16)
+        nc.vector.memset(ones[:], 1.0)
 
         ident = const.tile([P, P], F32)
         make_identity(nc, ident[:])
@@ -100,22 +104,23 @@ def tile_swintransformerblock_pa_kernel(
         nc.vector.tensor_copy(out=swap[:, :, :, 0, :], in_=same[:, :, :, 1, :])
         nc.vector.tensor_copy(out=swap[:, :, :, 1, :], in_=same[:, :, :, 0, :])
 
-        x_codes = const.tile([P, N_QUADS, PASSES, QUAD * P], U32, align_bytes=64)
-        x_scales = const.tile([P, N_QUADS, PASSES, QUAD * P], U8, align_bytes=64)
+        x_codes = const.tile([P, N_PAIRS, PASSES, PAIR * P], U32, align_bytes=64)
+        x_scales = const.tile([P, N_PAIRS, PASSES, PAIR * P], U8, align_bytes=64)
         w_codes = [
-            const.tile([P, PASSES, W_ROWS], U32, name="w_codes%d" % n, align_bytes=64)
-            for n in range(N_CHUNKS)
+            const.tile([P, PASSES, N_COLS], U32, name="w_codes%d" % s, align_bytes=64)
+            for s in range(N_SLABS)
         ]
         w_scales = [
-            const.tile([P, PASSES, W_ROWS], U8, name="w_scales%d" % n, align_bytes=64)
-            for n in range(N_CHUNKS)
+            const.tile([P, PASSES, N_COLS], U8, name="w_scales%d" % s, align_bytes=64)
+            for s in range(N_SLABS)
         ]
         mean_var = const.tile([P, WS, 2], F32)
         std = const.tile([P, WS], F32)
         neg_mean = const.tile([P, WS], F32)
         rstd = const.tile([P, WS], F32)
-        planes = [const.tile([P, PLANES, QUAD * P], BF16, name="planes%d" % h) for h in range(N_QUADS)]
+        planes = [const.tile([P, PLANES, PAIR * P], BF16, name="planes%d" % q) for q in range(N_PAIRS)]
         centred = {}
+        flipped = {}
         grouped = {}
         w_grouped = {}
 
@@ -128,7 +133,7 @@ def tile_swintransformerblock_pa_kernel(
                 )
             nc.vector.bn_aggr(out=mean_var[:, c, :], in_=stats[:].rearrange("p h s -> p (h s)"))
             nc.scalar.activation(
-                out=std[:, c : c + 1], in_=mean_var[:, c, 1:2], func=ACT.Sqrt, bias=eps[:, 0:1], scale=1.0
+                out=std[:, c : c + 1], in_=mean_var[:, c, 1:2], func=ACT.Sqrt, bias=EPS, scale=1.0
             )
             nc.scalar.activation(
                 out=neg_mean[:, c : c + 1], in_=mean_var[:, c, 0:1], func=ACT.Identity, scale=-1.0
@@ -136,11 +141,11 @@ def tile_swintransformerblock_pa_kernel(
 
         def centre(c):
             nc.vector.reciprocal(out=rstd[:, c : c + 1], in_=std[:, c : c + 1])
-            h, i = divmod(c, QUAD)
+            q, i = divmod(c, PAIR)
             if i == 0:
-                centred[h] = work.tile([P, QUAD, C], F32, name="centred")
+                centred[q] = centred_pool.tile([P, PAIR, C], F32, name="centred")
             nc.gpsimd.tensor_scalar(
-                out=centred[h][:, i, :].rearrange("p (a e k) -> p a e k", a=QUARTERS, e=2),
+                out=centred[q][:, i, :].rearrange("p (a e k) -> p a e k", a=QUARTERS, e=2),
                 in0=x_raw[:, tile_of(c), :].rearrange("p (a k e) -> p a e k", a=QUARTERS, e=2),
                 scalar1=neg_mean[:, c : c + 1],
                 scalar2=rstd[:, c : c + 1],
@@ -148,72 +153,78 @@ def tile_swintransformerblock_pa_kernel(
                 op1=ALU.mult,
             )
 
-        def flip_tokens(h, a):
-            for e in range(2):
-                plane = 2 * a + e
-                bank = psum.tile([P, QUAD, P], F32, tag="bank", name="flipped")
-                for i in range(QUAD):
-                    nc.tensor.transpose(
-                        out=bank[:, i, :],
-                        in_=centred[h][:, i, P * plane : P * (plane + 1)],
-                        identity=(roll_same if QUAD * h + i < WS - SHIFT else roll_swap)[:],
-                    )
-                nc.scalar.activation(
-                    out=planes[h][:, plane, :],
-                    in_=bank[:].rearrange("p i m -> p (i m)"),
-                    func=ACT.Identity,
-                    scale=gain[:, plane : plane + 1],
-                    bias=beta[:, plane : plane + 1],
-                )
+        def flip_tokens(q, g):
+            flipped[q, g] = []
+            for u in range(2):
+                bank = psum.tile([P, 2, PAIR, P], F32, tag="bank", name="flipped")
+                for e in range(2):
+                    plane = PACK * g + 2 * u + e
+                    for i in range(PAIR):
+                        nc.tensor.transpose(
+                            out=bank[:, e, i, :],
+                            in_=centred[q][:, i, P * plane : P * (plane + 1)],
+                            identity=(roll_same if PAIR * q + i < WS - SHIFT else roll_swap)[:],
+                        )
+                flipped[q, g].append(bank)
 
-        def regroup_tokens(h, g):
+        def scale_tokens(q, g):
+            for u in range(2):
+                for e in range(2):
+                    plane = PACK * g + 2 * u + e
+                    nc.scalar.activation(
+                        out=planes[q][:, plane, :],
+                        in_=flipped[q, g][u][:, e, :, :].rearrange("p i m -> p (i m)"),
+                        func=ACT.Identity,
+                        scale=gain[:, plane : plane + 1],
+                        bias=beta[:, plane : plane + 1],
+                    )
+
+        def regroup_tokens(q, g):
             if g == 0:
-                grouped[h] = work.tile([P, PASSES, QUAD * P, PACK], BF16, name="grouped", align_bytes=64)
+                grouped[q] = work.tile([P, PASSES, PAIR * P, PACK], BF16, name="grouped", align_bytes=64)
             nc.vector.tensor_copy(
-                out=grouped[h][:, g, :, :].rearrange("p (m i) t -> p m t i", i=4),
-                in_=planes[h][:, PACK * g : PACK * (g + 1), :].rearrange("p t (m i) -> p m t i", i=4),
+                out=grouped[q][:, g, :, :].rearrange("p (m i) t -> p m t i", i=4),
+                in_=planes[q][:, PACK * g : PACK * (g + 1), :].rearrange("p t (m i) -> p m t i", i=4),
             )
 
-        def quantise_tokens(h, g):
+        def quantise_tokens(q, g):
             nc.vector.quantize_mx(
-                out=x_codes[:, h, g, :].bitcast(FP8X4),
-                scales=x_scales[:, h, g, :],
-                in_=grouped[h][:, g, :, :].rearrange("p m t -> p (m t)"),
+                out=x_codes[:, q, g, :].bitcast(FP8X4),
+                scales=x_scales[:, q, g, :],
+                in_=grouped[q][:, g, :, :].rearrange("p m t -> p (m t)"),
             )
 
-        def flip_weights(n):
-            words = w_raw[n][:].bitcast(F32)
-            w_grouped[n] = work.tile([P, PASSES, W_ROWS, PACK], BF16, name="w_grouped", align_bytes=64)
-            grouped_words = w_grouped[n][:].bitcast(F32)
+        def flip_weights(s):
+            words = w_raw[s][:].bitcast(F32)
+            w_grouped[s] = slab_pool.tile([P, PASSES, N_COLS, PACK], BF16, name="w_grouped", align_bytes=64)
+            grouped_words = w_grouped[s][:].bitcast(F32)
             for g in range(PASSES):
-                for half in range(2):
-                    bank = psum.tile([P, 2, 2 * P], F32, tag="bank", name="w_flipped")
-                    for u in range(2):
-                        for jj in range(2):
-                            a = 2 * g + u
-                            nc.tensor.transpose(
-                                out=bank[:, u, P * jj : P * (jj + 1)],
-                                in_=words[:, 2 * half + jj, P * a : P * (a + 1)],
-                                identity=ident[:],
-                            )
-                    nc.scalar.copy(
-                        out=grouped_words[:, g, 2 * P * half : 2 * P * (half + 1), :],
-                        in_=bank[:].rearrange("p u c -> p c u"),
-                    )
+                bank = psum.tile([P, 2, N_COLS], F32, tag="bank", name="w_flipped")
+                for u in range(2):
+                    for j in range(ROW_TILES):
+                        a = 2 * g + u
+                        nc.tensor.transpose(
+                            out=bank[:, u, P * j : P * (j + 1)],
+                            in_=words[:, j, P * a : P * (a + 1)],
+                            identity=ident[:],
+                        )
+                nc.scalar.copy(out=grouped_words[:, g, :, :], in_=bank[:].rearrange("p u c -> p c u"))
+            cols = slice(N_COLS * s, N_COLS * (s + 1))
+            spread = psum.tile([P, N_COLS], F32, tag="bank")
+            nc.tensor.matmul(out=spread[:], lhsT=ones[:], rhs=bias_row[:, cols], start=True, stop=True)
+            nc.scalar.copy(out=bias_all[:, cols], in_=spread[:])
 
-        def quantise_weights(n):
+        def quantise_weights(s):
             nc.vector.quantize_mx(
-                out=w_codes[n][:].rearrange("p g c -> p (g c)").bitcast(FP8X4),
-                scales=w_scales[n][:].rearrange("p g c -> p (g c)"),
-                in_=w_grouped[n][:].rearrange("p g c t -> p (g c t)"),
+                out=w_codes[s][:].rearrange("p g c -> p (g c)").bitcast(FP8X4),
+                scales=w_scales[s][:].rearrange("p g c -> p (g c)"),
+                in_=w_grouped[s][:].rearrange("p g c t -> p (g c t)"),
             )
 
-        def project(n, half):
+        def project(s):
             stage = stage_pool.tile([P, HEADS, WS, HD], F32)
-            cols = slice(N_COLS * half, N_COLS * (half + 1))
-            first_col = W_ROWS * n + N_COLS * half
             bias = (
-                bias_all[:, first_col : first_col + N_COLS]
+                bias_all[:, N_COLS * s : N_COLS * (s + 1)]
                 .rearrange("p (a d) -> p a d", d=HD)
                 .unsqueeze(2)
                 .to_broadcast([P, HEADS, PAIR, HD])
@@ -221,56 +232,57 @@ def tile_swintransformerblock_pa_kernel(
             for q in range(N_PAIRS):
                 acc = psum.tile([P, PAIR, N_COLS], F32, tag="bank")
                 for i in range(PAIR):
-                    h, tile_in_quad = divmod(PAIR * q + i, QUAD)
-                    tokens = slice(P * tile_in_quad, P * (tile_in_quad + 1))
+                    tokens = slice(P * i, P * (i + 1))
                     for g in range(PASSES):
                         nc.tensor.matmul_mx(
                             out=acc[:, i, :],
-                            lhsT=x_codes[:, h, g, tokens].bitcast(FP8X4),
-                            lhsT_scale=x_scales[:, h, g, tokens],
-                            rhs=w_codes[n][:, g, cols].bitcast(FP8X4),
-                            rhs_scale=w_scales[n][:, g, cols],
+                            lhsT=x_codes[:, q, g, tokens].bitcast(FP8X4),
+                            lhsT_scale=x_scales[:, q, g, tokens],
+                            rhs=w_codes[s][:, g, :].bitcast(FP8X4),
+                            rhs_scale=w_scales[s][:, g, :],
                             start=(g == 0),
                             stop=(g == PASSES - 1),
                         )
-                by_head = acc[:].rearrange("p i (a d) -> p a i d", d=HD)
-                place = stage[:, :, PAIR * q : PAIR * (q + 1), :]
-                if q < PAIR - half:
-                    nc.scalar.copy(out=place, in_=by_head)
-                    nc.gpsimd.tensor_tensor(out=place, in0=place, in1=bias, op=ALU.add)
-                else:
-                    nc.vector.tensor_tensor(out=place, in0=by_head, in1=bias, op=ALU.add)
-            rows_of = outs[n // 2].rearrange("w a (r c) d -> a w r (c d)", c=WS)
-            first_head = (first_col % C) // HD
+                nc.vector.tensor_tensor(
+                    out=stage[:, :, PAIR * q : PAIR * (q + 1), :],
+                    in0=acc[:].rearrange("p i (a d) -> p a i d", d=HD),
+                    in1=bias,
+                    op=ALU.add,
+                )
+            slabs_per_output = C // N_COLS
+            rows_of = outs[s // slabs_per_output].rearrange("w a (r c) d -> a w r (c d)", c=WS)
+            first_head = HEADS * (s % slabs_per_output)
             for a in range(HEADS):
                 nc.sync.dma_start(
                     out=rows_of[first_head + a], in_=stage[:, a, :, :].rearrange("p c d -> p (c d)")
                 )
 
-        for step in range(WS + FLIP_LAG):
+        for step in range(WS + SCALE_LAG):
             if step < WS:
                 statistics(step)
             if 1 <= step <= WS:
                 centre(step - 1)
-            if step == FLIP_LAG - 2:
-                flip_weights(0)
-            if step == FLIP_LAG - 1:
-                flip_weights(1)
+            if 1 <= step < FLIP_LAG:
+                flip_weights(step - 1)
+            if step == FLIP_LAG:
                 nc.vector.tensor_copy(out=gain[:], in_=gain_bf[:].rearrange("p a e -> p (a e)"))
                 nc.vector.tensor_copy(out=beta[:], in_=beta_bf[:].rearrange("p a e -> p (a e)"))
-            if step >= FLIP_LAG:
-                flip_tokens(*divmod(step - FLIP_LAG, QUARTERS))
+            if 0 <= step - FLIP_LAG < WS:
+                flip_tokens(*divmod(step - FLIP_LAG, PASSES))
+            if 0 <= step - SCALE_LAG < WS:
+                scale_tokens(*divmod(step - SCALE_LAG, PASSES))
         quantise_weights(0)
-        quantise_weights(1)
-        for h in range(N_QUADS):
-            for g in range(PASSES):
-                regroup_tokens(h, g)
-                quantise_tokens(h, g)
+        for unit in range(WS + 1):
+            if unit < WS:
+                regroup_tokens(*divmod(unit, PASSES))
+            if unit > 0:
+                quantise_tokens(*divmod(unit - 1, PASSES))
 
-        for n in range(N_CHUNKS):
-            project(n, 0)
-            if n + 2 < N_CHUNKS:
-                flip_weights(n + 2)
-            project(n, 1)
-            if n + 2 < N_CHUNKS:
-                quantise_weights(n + 2)
+        for s in range(0, N_SLABS, 2):
+            project(s)
+            quantise_weights(s + 1)
+            if s + 2 < N_SLABS:
+                flip_weights(s + 2)
+                flip_weights(s + 3)
+                quantise_weights(s + 2)
+            project(s + 1)

@@ -26,6 +26,7 @@ N_COLS = 256
 N_SLABS = 3 * C // N_COLS
 ROW_TILES = N_COLS // P
 HEADS = N_COLS // HD
+GPSIMD_HEADS = 2
 BANKS = 8
 FLIP_LAG = 3
 SCALE_LAG = 4
@@ -253,7 +254,8 @@ def tile_swintransformerblock_pa_kernel(
             rows_of = outs[s // slabs_per_output].rearrange("w a (r c) d -> a w r (c d)", c=WS)
             first_head = HEADS * (s % slabs_per_output)
             for a in range(HEADS):
-                nc.sync.dma_start(
+                queue = nc.sync if a < HEADS - GPSIMD_HEADS else nc.gpsimd
+                queue.dma_start(
                     out=rows_of[first_head + a], in_=stage[:, a, :, :].rearrange("p c d -> p (c d)")
                 )
 

@@ -26,7 +26,6 @@ N_COLS = 256
 N_SLABS = 3 * C // N_COLS
 ROW_TILES = N_COLS // P
 HEADS = N_COLS // HD
-GPSIMD_HEADS = 2
 BANKS = 8
 FLIP_LAG = 3
 SCALE_LAG = 4
@@ -244,18 +243,18 @@ def tile_swintransformerblock_pa_kernel(
                             start=(g == 0),
                             stop=(g == PASSES - 1),
                         )
-                nc.vector.tensor_tensor(
-                    out=stage[:, :, PAIR * q : PAIR * (q + 1), :],
-                    in0=acc[:].rearrange("p i (a d) -> p a i d", d=HD),
-                    in1=bias,
-                    op=ALU.add,
-                )
+                by_head = acc[:].rearrange("p i (a d) -> p a i d", d=HD)
+                place = stage[:, :, PAIR * q : PAIR * (q + 1), :]
+                if q < PAIR - s % 2:
+                    nc.scalar.copy(out=place, in_=by_head)
+                    nc.gpsimd.tensor_tensor(out=place, in0=place, in1=bias, op=ALU.add)
+                else:
+                    nc.vector.tensor_tensor(out=place, in0=by_head, in1=bias, op=ALU.add)
             slabs_per_output = C // N_COLS
             rows_of = outs[s // slabs_per_output].rearrange("w a (r c) d -> a w r (c d)", c=WS)
             first_head = HEADS * (s % slabs_per_output)
             for a in range(HEADS):
-                queue = nc.sync if a < HEADS - GPSIMD_HEADS else nc.gpsimd
-                queue.dma_start(
+                nc.sync.dma_start(
                     out=rows_of[first_head + a], in_=stage[:, a, :, :].rearrange("p c d -> p (c d)")
                 )
 

from contextlib import ExitStack

import concourse.mybir as mybir
from concourse.masks import make_identity

F32 = mybir.dt.float32
BF16 = mybir.dt.bfloat16
U32 = mybir.dt.uint32
U8 = mybir.dt.uint8
FP8X4 = mybir.dt.float8_e4m3fn_x4
ALU = mybir.AluOpType
ACT = mybir.ActivationFunctionType

P = 128
C = 1024
EPS = 1e-5
IMAGES, GRID, WS, SHIFT = 4, 16, 8, 3
HD = 32
PACK = 4
PASSES = C // (P * PACK)
QUARTERS = C // (2 * P)
PLANES = C // P
PAIR = 2
N_PAIRS = WS // PAIR
N_COLS = 256
N_SLABS = 3 * C // N_COLS
ROW_TILES = N_COLS // P
HEADS = N_COLS // HD
BANKS = 8
FLIP_LAG = 3
SCALE_LAG = 4

FLOPS = 2 * IMAGES * GRID * GRID * C * 3 * C


def tile_swintransformerblock_pa_kernel(
    tc, x, norm1_w, norm1_b, qkv_w, qkv_b, out_0, out_1, out_2
):
    nc = tc.nc
    outs = (out_0, out_1, out_2)

    with ExitStack() as ctx:
        ctx.enter_context(tc.manual_schedule())
        const = ctx.enter_context(tc.tile_pool(name="const", bufs=1))
        small = ctx.enter_context(tc.tile_pool(name="small", bufs=4))
        centred_pool = ctx.enter_context(tc.tile_pool(name="centred", bufs=3))
        work = ctx.enter_context(tc.tile_pool(name="work", bufs=2))
        slab_pool = ctx.enter_context(tc.tile_pool(name="slab", bufs=4))
        stage_pool = ctx.enter_context(tc.tile_pool(name="stage", bufs=4))
        psum = ctx.enter_context(tc.psum_pool(name="psum", bufs=BANKS))

        x_raw = const.tile([P, WS, C], BF16)
        x_rows = x.rearrange("b (q e) k -> (b q) e k", e=WS)
        w_raw = [const.tile([P, ROW_TILES, C], BF16, name="w_raw%d" % s) for s in range(N_SLABS)]
        bias_row = const.tile([P, 3 * C], BF16)
        nc.gpsimd.memset(bias_row[:].bitcast(F32), 0.0)
        bias_all = const.tile([P, 3 * C], F32)

        def tile_of(c):
            return (c + SHIFT) % WS

        def load_tokens(first, last):
            nc.sync.dma_start(out=x_raw[:, first:last, :], in_=x_rows[:, first:last, :])

        def load_weights(s):
            rows = qkv_w[N_COLS * s : N_COLS * (s + 1), :]
            nc.sync.dma_start(out=w_raw[s][:], in_=rows.rearrange("(j p) k -> p j k", p=P))

        load_tokens(SHIFT, SHIFT + 1)
        load_tokens(SHIFT + 1, SHIFT + 3)
        load_weights(0)
        load_tokens(SHIFT + 3, WS)
        load_weights(1)
        load_tokens(0, SHIFT)
        for s in range(2, N_SLABS):
            load_weights(s)

        gain_bf = const.tile([P, QUARTERS, 2], BF16)
        beta_bf = const.tile([P, QUARTERS, 2], BF16)
        with nc.allow_non_contiguous_dma(reason="two small vectors, one pair of channels a piece"):
            nc.scalar.dma_start(out=gain_bf[:], in_=norm1_w.rearrange("(a p e) -> p a e", p=P, e=2))
            nc.scalar.dma_start(out=beta_bf[:], in_=norm1_b.rearrange("(a p e) -> p a e", p=P, e=2))
        nc.scalar.dma_start(out=bias_row[0:1, :], in_=qkv_b.rearrange("(o n) -> o n", o=1))
        gain = const.tile([P, PLANES], F32)
        beta = const.tile([P, PLANES], F32)

        warm = const.tile([P, 2], F32)
        nc.vector.memset(warm[:, 0:1], 1.0)
        nc.scalar.activation(out=warm[:, 1:2], in_=warm[:, 0:1], func=ACT.Sqrt)
        ones = const.tile([P, P], BF16)
        nc.vector.memset(ones[:], 1.0)

        ident = const.tile([P, P], F32)
        make_identity(nc, ident[:])
        by_grid = ident[:].rearrange("p (b i h) -> p b h i", b=IMAGES, h=2)
        roll_same = const.tile([P, P], F32)
        same = roll_same[:].rearrange("p (b wi wj r) -> p b wi wj r", b=IMAGES, wi=2, wj=2)
        wrap = GRID - WS - SHIFT
        nc.vector.tensor_copy(out=same[:, :, 0, :, :], in_=by_grid[:, :, :, SHIFT : SHIFT + WS])
        nc.vector.tensor_copy(out=same[:, :, 1, :, 0:wrap], in_=by_grid[:, :, :, SHIFT + WS : GRID])
        nc.vector.tensor_copy(out=same[:, :, 1, :, wrap:WS], in_=by_grid[:, :, :, 0:SHIFT])
        roll_swap = const.tile([P, P], F32)
        swap = roll_swap[:].rearrange("p (b wi wj r) -> p b wi wj r", b=IMAGES, wi=2, wj=2)
        nc.vector.tensor_copy(out=swap[:, :, :, 0, :], in_=same[:, :, :, 1, :])
        nc.vector.tensor_copy(out=swap[:, :, :, 1, :], in_=same[:, :, :, 0, :])

        x_codes = const.tile([P, N_PAIRS, PASSES, PAIR * P], U32, align_bytes=64)
        x_scales = const.tile([P, N_PAIRS, PASSES, PAIR * P], U8, align_bytes=64)
        w_codes = [
            const.tile([P, PASSES, N_COLS], U32, name="w_codes%d" % s, align_bytes=64)
            for s in range(N_SLABS)
        ]
        w_scales = [
            const.tile([P, PASSES, N_COLS], U8, name="w_scales%d" % s, align_bytes=64)
            for s in range(N_SLABS)
        ]
        mean_var = const.tile([P, WS, 2], F32)
        std = const.tile([P, WS], F32)
        neg_mean = const.tile([P, WS], F32)
        rstd = const.tile([P, WS], F32)
        planes = [const.tile([P, PLANES, PAIR * P], BF16, name="planes%d" % q) for q in range(N_PAIRS)]
        centred = {}
        flipped = {}
        grouped = {}
        w_grouped = {}

        def statistics(c):
            stats = small.tile([P, 2, 6], F32)
            for half in range(2):
                nc.vector.bn_stats(
                    out=stats[:, half, :],
                    in_=x_raw[:, tile_of(c), (C // 2) * half : (C // 2) * (half + 1)],
                )
            nc.vector.bn_aggr(out=mean_var[:, c, :], in_=stats[:].rearrange("p h s -> p (h s)"))
            nc.scalar.activation(
                out=std[:, c : c + 1], in_=mean_var[:, c, 1:2], func=ACT.Sqrt, bias=EPS, scale=1.0
            )
            nc.scalar.activation(
                out=neg_mean[:, c : c + 1], in_=mean_var[:, c, 0:1], func=ACT.Identity, scale=-1.0
            )

        def centre(c):
            nc.vector.reciprocal(out=rstd[:, c : c + 1], in_=std[:, c : c + 1])
            q, i = divmod(c, PAIR)
            if i == 0:
                centred[q] = centred_pool.tile([P, PAIR, C], F32, name="centred")
            nc.gpsimd.tensor_scalar(
                out=centred[q][:, i, :].rearrange("p (a e k) -> p a e k", a=QUARTERS, e=2),
                in0=x_raw[:, tile_of(c), :].rearrange("p (a k e) -> p a e k", a=QUARTERS, e=2),
                scalar1=neg_mean[:, c : c + 1],
                scalar2=rstd[:, c : c + 1],
                op0=ALU.add,
                op1=ALU.mult,
            )

        def flip_tokens(q, g):
            flipped[q, g] = []
            for u in range(2):
                bank = psum.tile([P, 2, PAIR, P], F32, tag="bank", name="flipped")
                for e in range(2):
                    plane = PACK * g + 2 * u + e
                    for i in range(PAIR):
                        nc.tensor.transpose(
                            out=bank[:, e, i, :],
                            in_=centred[q][:, i, P * plane : P * (plane + 1)],
                            identity=(roll_same if PAIR * q + i < WS - SHIFT else roll_swap)[:],
                        )
                flipped[q, g].append(bank)

        def scale_tokens(q, g):
            for u in range(2):
                for e in range(2):
                    plane = PACK * g + 2 * u + e
                    nc.scalar.activation(
                        out=planes[q][:, plane, :],
                        in_=flipped[q, g][u][:, e, :, :].rearrange("p i m -> p (i m)"),
                        func=ACT.Identity,
                        scale=gain[:, plane : plane + 1],
                        bias=beta[:, plane : plane + 1],
                    )

        def regroup_tokens(q, g):
            if g == 0:
                grouped[q] = work.tile([P, PASSES, PAIR * P, PACK], BF16, name="grouped", align_bytes=64)
            nc.vector.tensor_copy(
                out=grouped[q][:, g, :, :].rearrange("p (m i) t -> p m t i", i=4),
                in_=planes[q][:, PACK * g : PACK * (g + 1), :].rearrange("p t (m i) -> p m t i", i=4),
            )

        def quantise_tokens(q, g):
            nc.vector.quantize_mx(
                out=x_codes[:, q, g, :].bitcast(FP8X4),
                scales=x_scales[:, q, g, :],
                in_=grouped[q][:, g, :, :].rearrange("p m t -> p (m t)"),
            )

        def flip_weights(s):
            words = w_raw[s][:].bitcast(F32)
            w_grouped[s] = slab_pool.tile([P, PASSES, N_COLS, PACK], BF16, name="w_grouped", align_bytes=64)
            grouped_words = w_grouped[s][:].bitcast(F32)
            for g in range(PASSES):
                bank = psum.tile([P, 2, N_COLS], F32, tag="bank", name="w_flipped")
                for u in range(2):
                    for j in range(ROW_TILES):
                        a = 2 * g + u
                        nc.tensor.transpose(
                            out=bank[:, u, P * j : P * (j + 1)],
                            in_=words[:, j, P * a : P * (a + 1)],
                            identity=ident[:],
                        )
                nc.scalar.copy(out=grouped_words[:, g, :, :], in_=bank[:].rearrange("p u c -> p c u"))
            cols = slice(N_COLS * s, N_COLS * (s + 1))
            spread = psum.tile([P, N_COLS], F32, tag="bank")
            nc.tensor.matmul(out=spread[:], lhsT=ones[:], rhs=bias_row[:, cols], start=True, stop=True)
            nc.scalar.copy(out=bias_all[:, cols], in_=spread[:])

        def quantise_weights(s):
            nc.vector.quantize_mx(
                out=w_codes[s][:].rearrange("p g c -> p (g c)").bitcast(FP8X4),
                scales=w_scales[s][:].rearrange("p g c -> p (g c)"),
                in_=w_grouped[s][:].rearrange("p g c t -> p (g c t)"),
            )

        def project(s):
            stage = stage_pool.tile([P, HEADS, WS, HD], F32)
            bias = (
                bias_all[:, N_COLS * s : N_COLS * (s + 1)]
                .rearrange("p (a d) -> p a d", d=HD)
                .unsqueeze(2)
                .to_broadcast([P, HEADS, PAIR, HD])
            )
            for q in range(N_PAIRS):
                acc = psum.tile([P, PAIR, N_COLS], F32, tag="bank")
                for i in range(PAIR):
                    tokens = slice(P * i, P * (i + 1))
                    for g in range(PASSES):
                        nc.tensor.matmul_mx(
                            out=acc[:, i, :],
                            lhsT=x_codes[:, q, g, tokens].bitcast(FP8X4),
                            lhsT_scale=x_scales[:, q, g, tokens],
                            rhs=w_codes[s][:, g, :].bitcast(FP8X4),
                            rhs_scale=w_scales[s][:, g, :],
                            start=(g == 0),
                            stop=(g == PASSES - 1),
                        )
                by_head = acc[:].rearrange("p i (a d) -> p a i d", d=HD)
                place = stage[:, :, PAIR * q : PAIR * (q + 1), :]
                if q < PAIR - s % 2:
                    nc.scalar.copy(out=place, in_=by_head)
                    nc.gpsimd.tensor_tensor(out=place, in0=place, in1=bias, op=ALU.add)
                else:
                    nc.vector.tensor_tensor(out=place, in0=by_head, in1=bias, op=ALU.add)
            slabs_per_output = C // N_COLS
            rows_of = outs[s // slabs_per_output].rearrange("w a (r c) d -> a w r (c d)", c=WS)
            first_head = HEADS * (s % slabs_per_output)
            for a in range(HEADS):
                nc.sync.dma_start(
                    out=rows_of[first_head + a], in_=stage[:, a, :, :].rearrange("p c d -> p (c d)")
                )

        for step in range(WS + SCALE_LAG):
            if step < WS:
                statistics(step)
            if 1 <= step <= WS:
                centre(step - 1)
            if 1 <= step < FLIP_LAG:
                flip_weights(step - 1)
            if step == FLIP_LAG:
                nc.vector.tensor_copy(out=gain[:], in_=gain_bf[:].rearrange("p a e -> p (a e)"))
                nc.vector.tensor_copy(out=beta[:], in_=beta_bf[:].rearrange("p a e -> p (a e)"))
            if 0 <= step - FLIP_LAG < WS:
                flip_tokens(*divmod(step - FLIP_LAG, PASSES))
            if 0 <= step - SCALE_LAG < WS:
                scale_tokens(*divmod(step - SCALE_LAG, PASSES))
        quantise_weights(0)
        for unit in range(WS + 1):
            if unit < WS:
                regroup_tokens(*divmod(unit, PASSES))
            if unit > 0:
                quantise_tokens(*divmod(unit - 1, PASSES))

        for s in range(0, N_SLABS, 2):
            project(s)
            quantise_weights(s + 1)
            if s + 2 < N_SLABS:
                flip_weights(s + 2)
                flip_weights(s + 3)
                quantise_weights(s + 2)
            project(s + 1)
